import numpy as np
import ml_dtypes


def mxq(x, axis, fmt="e4m3"):
    dtype, down = {"e4m3": (ml_dtypes.float8_e4m3fn, 7), "e5m2": (ml_dtypes.float8_e5m2, 14)}[fmt]
    v = np.moveaxis(np.asarray(x, np.float32).astype(ml_dtypes.bfloat16).astype(np.float64), axis, -1)
    blocks = v.reshape(v.shape[:-1] + (-1, 32))
    amax = np.abs(blocks).max(-1, keepdims=True)
    byte = np.maximum(np.where(amax > 0, np.frexp(amax)[1] - 1 + 127, 0) - down, 1)
    scale = np.exp2(byte - 127.0)
    codes = (blocks / scale).astype(np.float32).astype(dtype).astype(np.float64)
    return np.moveaxis((codes * scale).reshape(v.shape), -1, axis)


WIDE = False


def mx_kscale(k):
    if not WIDE:
        return np.ones(k)
    levels = np.array([10, -10, 5, -5, 0])
    a = np.random.permutation(np.resize(levels, k // 512 * 4)).reshape(k // 512, 4)
    idx = np.arange(k)
    return np.exp2(a[idx // 512, idx % 128 // 32])


BF16 = ml_dtypes.bfloat16


def bf(x):
    return np.asarray(x, np.float32).astype(BF16)


def f64(x):
    return np.asarray(x).astype(np.float64)


B, L, D, F = 4, 1024, 512, 512


def silu(z):
    return z / (1.0 + np.exp(-z))


def sigmoid(z):
    return 1.0 / (1.0 + np.exp(-z))


def setup_inputs():
    s = mx_kscale(D)
    return {
        "x": bf(np.random.standard_normal((B, L, D)) * s),
        "W1": bf(np.random.standard_normal((D, F)) / np.sqrt(D) / s[:, None]),
        "b1": bf(np.random.standard_normal(F) * 0.3),
        "W2g": bf(np.random.standard_normal((F, D)) * 2.4 / np.sqrt(F)),
        "b2g": bf(np.random.standard_normal(D) * 0.3),
        "Wv": bf(np.random.standard_normal((D, D)) * 1.8 / np.sqrt(D) / s[:, None]),
        "bv": bf(np.random.standard_normal(D) * 0.3),
    }


def reference(x, W1, b1, W2g, b2g, Wv, bv):
    xq = mxq(f64(x), 2, "e4m3")
    h = silu((xq @ mxq(f64(W1), 0, "e4m3")) + f64(b1))
    g = (mxq(h, 2, "e4m3") @ mxq(f64(W2g), 0, "e4m3")) + f64(b2g)
    return ((xq @ mxq(f64(Wv), 0, "e4m3")) + f64(bv)) * sigmoid(g)

@@ -1,0 +1,383 @@
+from contextlib import ExitStack
+
+import concourse.mybir as mybir
+from concourse.masks import make_identity
+
+F32 = mybir.dt.float32
+BF16 = mybir.dt.bfloat16
+U32 = mybir.dt.uint32
+U8 = mybir.dt.uint8
+FP8X4 = mybir.dt.float8_e4m3fn_x4
+ACT = mybir.ActivationFunctionType
+ALU = mybir.AluOpType
+
+P = 128
+PACK = 4
+DIM = 512
+TOKENS = 4096
+BLK = 512
+NB = TOKENS // BLK
+FLOPS = 3 * 2 * TOKENS * DIM * DIM
+
+XG_BUFS = 3
+HG_BUFS = 2
+SIG_BUFS = 4
+OT_BUFS = 2
+OSB_BUFS = 3
+XT_BANKS = (0, 1, 2, 3)
+Z_BANKS = (4, 5, 6, 7)
+XC_ON_ACT = ((0, 0), (0, 1), (1, 0), (1, 1))
+EV_ON_DVE = ((2, 3), (3, 1), (3, 3), (4, 1), (4, 3), (5, 1), (5, 3), (6, 1), (6, 3), (7, 1), (7, 3))
+H_EARLY = 5
+
+
+def tile_selectivemixing_pa_t_kernel(tc, x, W1, b1, W2g, b2g, Wv, bv, out):
+    nc = tc.nc
+    xf = x.flatten_outer_dims()
+    of = out.flatten_outer_dims()
+    steps = {}
+    order = {"SP": [], "POOL": [], "PE": [], "DVE": [], "ACT": []}
+
+    def step(engine, name, deps, fn):
+        steps[name] = (deps, fn)
+        order[engine].append(name)
+
+    with ExitStack() as ctx:
+        keep = ctx.enter_context(tc.tile_pool(name="keep", bufs=1))
+        ring = ctx.enter_context(tc.tile_pool(name="ring", bufs=1))
+        psum = ctx.enter_context(tc.psum_pool(name="psum", bufs=1))
+        ctx.enter_context(tc.manual_schedule())
+
+        ident = keep.tile([P, P], F32, name="ident")
+        warm = keep.tile([P, 2], F32, name="warm")
+        b1raw = keep.tile([P, PACK], BF16, name="b1raw")
+        b1f = keep.tile([P, PACK], F32, name="b1f")
+        brow = keep.tile([P, P], BF16, name="brow")
+        browf = keep.tile([P, P], F32, name="browf")
+        b2v = keep.tile([P, 8], F32, name="b2v")
+        wraw = {}
+        wgrp = {}
+        wcod = {}
+        wscl = {}
+        for w in ("w1", "wv", "w2"):
+            wraw[w] = keep.tile([P, PACK, DIM], BF16, name=w + "raw")
+            wgrp[w] = keep.tile([P, DIM * PACK], BF16, name=w + "grp", align_bytes=64)
+            wcod[w] = keep.tile([P, DIM], U32, name=w + "cod", align_bytes=64)
+            wscl[w] = keep.tile([P, DIM], U8, name=w + "scl", align_bytes=64)
+        xcod = keep.tile([P, TOKENS], U32, name="xcod", align_bytes=64)
+        xscl = keep.tile([P, TOKENS], U8, name="xscl", align_bytes=64)
+        hcod = keep.tile([P, TOKENS], U32, name="hcod", align_bytes=64)
+        hscl = keep.tile([P, TOKENS], U8, name="hscl", align_bytes=64)
+        xsb = [keep.tile([P, PACK * DIM], BF16, name="xsb%d" % b) for b in range(NB)]
+        hraw = [keep.tile([P, PACK, BLK], BF16, name="hraw%d" % b) for b in range(NB)]
+        live = {}
+
+        def ring_tile(key, shape, dtype, tag, bufs, align=None):
+            if key not in live:
+                live[key] = ring.tile(shape, dtype, name="%s_%s" % key, tag=tag, bufs=bufs, align_bytes=align)
+            return live[key]
+
+        def bank_tile(key, bank, shape):
+            live[key] = psum.tile(shape, F32, name="ps_%s_%s" % key, tag="bank%d" % bank)
+            return live[key]
+
+        last_reader = {}
+
+        def claim(bank, reader):
+            prev = last_reader.get(bank)
+            last_reader[bank] = reader
+            return [prev] if prev else []
+
+        cols = lambda b: slice(b * BLK, (b + 1) * BLK)
+
+        def ld_x(b):
+            nc.sync.dma_start(
+                out=xsb[b][:].rearrange("p (j d) -> p j d", j=PACK), in_=xf[cols(b), :].rearrange("(p j) d -> p j d", j=PACK)
+            )
+
+        def ld_w_pairs(w, src):
+            nc.sync.dma_start(
+                out=wraw[w][:].rearrange("q (u e) c -> q u (e c)", u=2),
+                in_=src.rearrange("(u q e) c -> q u (e c)", u=2, e=2),
+            )
+
+        def ld_w_rows(w, src):
+            nc.sync.dma_start(out=wraw[w][:], in_=src.rearrange("(p j) c -> p j c", j=PACK))
+
+        def memsets():
+            nc.vector.memset(warm[:], 0.0)
+            nc.vector.memset(brow[:], 0.0)
+
+        def warm_table():
+            nc.scalar.activation(out=warm[:, 1:2], in_=warm[:, 0:1], func=ACT.Silu)
+
+        def ld_b1():
+            nc.sync.dma_start(out=b1raw[:], in_=b1.rearrange("(p t) -> p t", t=PACK))
+
+        def ld_bias():
+            nc.sync.dma_start(out=brow[0:4, :], in_=b2g.rearrange("(c p) -> c p", p=P))
+            nc.sync.dma_start(out=brow[4:8, :], in_=bv.rearrange("(c p) -> c p", p=P))
+
+        def regroup_w1(t):
+            nc.vector.tensor_copy(
+                out=wgrp["w1"][:, t * BLK:(t + 1) * BLK].rearrange("p (m k) -> p m k", k=PACK),
+                in_=wraw["w1"][:].rearrange("p k (m t) -> p t m k", t=PACK)[:, t],
+            )
+
+        def regroup_w(w):
+            nc.vector.tensor_copy(
+                out=wgrp[w][:].rearrange("p (c i k) -> p c k i", i=4, k=PACK),
+                in_=wraw[w][:].rearrange("p k (c i) -> p c k i", i=4),
+            )
+
+        def quant_w(w, lo, hi):
+            nc.vector.quantize_mx(
+                out=wcod[w][:, lo:hi].bitcast(FP8X4), scales=wscl[w][:, lo:hi], in_=wgrp[w][:, lo * PACK:hi * PACK]
+            )
+
+        def tx(b):
+            words = xsb[b][:].bitcast(F32)
+            for jj in range(2):
+                xt = bank_tile(("xt", 2 * b + jj), XT_BANKS[(2 * b + jj) % len(XT_BANKS)], [P, 2, 2 * P])
+                for jl in range(2):
+                    for u in range(2):
+                        w0 = ((2 * jj + jl) * 2 + u) * P
+                        nc.tensor.transpose(out=xt[:, u, jl * P:(jl + 1) * P], in_=words[:, w0:w0 + P], identity=ident[:])
+
+        def xc(b, jj, engine):
+            xg = ring_tile(("xg", b), [P, BLK * PACK], BF16, "xg", XG_BUFS, 64)
+            dst = xg[:].bitcast(F32)[:, jj * BLK:(jj + 1) * BLK].rearrange("p (c u) -> p c u", u=2)
+            src = live[("xt", 2 * b + jj)][:].rearrange("p u c -> p c u")
+            if engine == "ACT":
+                nc.scalar.copy(out=dst, in_=src)
+            else:
+                nc.vector.tensor_copy(out=dst, in_=src)
+
+        def qx(b):
+            nc.vector.quantize_mx(out=xcod[:, cols(b)].bitcast(FP8X4), scales=xscl[:, cols(b)], in_=live[("xg", b)][:])
+
+        def mx(key, bank, w, c, cod, scl, b):
+            acc = bank_tile(key, bank, [P, BLK])
+            nc.tensor.matmul_mx(
+                out=acc[:],
+                lhsT=wcod[w][:, c * P:(c + 1) * P].bitcast(FP8X4),
+                lhsT_scale=wscl[w][:, c * P:(c + 1) * P],
+                rhs=cod[:, cols(b)].bitcast(FP8X4),
+                rhs_scale=scl[:, cols(b)],
+                start=True,
+                stop=True,
+            )
+
+        def silu(b, t):
+            nc.scalar.activation(out=hraw[b][:, t, :], in_=live[("z", 4 * b + t)][:], func=ACT.Silu, bias=b1f[:, t:t + 1])
+
+        def hr(b):
+            hg = ring_tile(("hg", b), [P, BLK * PACK], BF16, "hg", HG_BUFS, 64)
+            nc.vector.tensor_copy(
+                out=hg[:].rearrange("p (c i k) -> p c k i", i=4, k=PACK),
+                in_=hraw[b][:].rearrange("p k (c i) -> p c k i", i=4),
+            )
+
+        def qh(b):
+            nc.vector.quantize_mx(out=hcod[:, cols(b)].bitcast(FP8X4), scales=hscl[:, cols(b)], in_=live[("hg", b)][:])
+
+        def sg(b, c):
+            s = ring_tile(("sig", 4 * b + c), [P, BLK], F32, "sig", SIG_BUFS)
+            nc.scalar.activation(out=s[:], in_=live[("g", 4 * b + c)][:], func=ACT.Sigmoid, bias=b2v[:, c:c + 1])
+
+        def st(b, c):
+            o = ring_tile(("ot", b), [P, PACK, BLK], F32, "ot", OT_BUFS)
+            nc.vector.scalar_tensor_tensor(
+                out=o[:, c, :], in0=live[("v", 4 * b + c)][:], scalar=b2v[:, 4 + c:5 + c], in1=live[("sig", 4 * b + c)][:],
+                op0=ALU.add, op1=ALU.mult,
+            )
+
+        def tout(b, j, bank):
+            acc = bank_tile(("o", 4 * b + j), bank, [P, DIM])
+            for c in range(4):
+                nc.tensor.transpose(out=acc[:, c * P:(c + 1) * P], in_=live[("ot", b)][:, c, j * P:(j + 1) * P], identity=ident[:])
+
+        def ev(b, j, engine):
+            o = ring_tile(("osb", b), [P, PACK, DIM], F32, "osb", OSB_BUFS)
+            if engine == "ACT":
+                nc.scalar.copy(out=o[:, j, :], in_=live[("o", 4 * b + j)][:])
+            else:
+                nc.vector.tensor_copy(out=o[:, j, :], in_=live[("o", 4 * b + j)][:])
+
+        def store(b, j0, j1):
+            nc.sync.dma_start(
+                out=of[cols(b), :].rearrange("(p j) d -> p j d", j=PACK)[:, j0:j1, :], in_=live[("osb", b)][:, j0:j1, :]
+            )
+
+        step("POOL", "ident", [], lambda: make_identity(nc, ident[:]))
+        step("SP", "ld_b1", [], ld_b1)
+        step("SP", "ld_x0", [], lambda: ld_x(0))
+        step("SP", "ld_w1", [], lambda: ld_w_pairs("w1", W1))
+        for b in range(1, NB):
+            step("SP", "ld_x%d" % b, [], lambda b=b: ld_x(b))
+        step("SP", "ld_wv", [], lambda: ld_w_pairs("wv", Wv))
+        step("SP", "ld_w2", [], lambda: ld_w_rows("w2", W2g))
+        step("SP", "ld_bias", ["memsets"], ld_bias)
+
+        step("DVE", "memsets", [], memsets)
+        step("ACT", "warm", ["memsets"], warm_table)
+
+        def pe_tx(b):
+            deps = ["ld_x%d" % b, "ident"]
+            for jj in range(2):
+                deps += claim(XT_BANKS[(2 * b + jj) % len(XT_BANKS)], "xc%d_%d" % (b, jj))
+            step("PE", "tx%d" % b, deps, lambda: tx(b))
+
+        def pe_mx1(b, ts=(0, 1, 2, 3)):
+            for t in ts:
+                bank = Z_BANKS[(4 * b + t) % len(Z_BANKS)]
+                deps = ["qx%d" % b, "qw1_%d" % (t // 2)] + claim(bank, "silu%d_%d" % (b, t))
+                step("PE", "mx1_%d_%d" % (b, t), deps, lambda t=t, bank=bank: mx(("z", 4 * b + t), bank, "w1", t, xcod, xscl, b))
+
+        pe_tx(0)
+        pe_tx(1)
+        pe_mx1(0, (0, 1))
+        pe_tx(2)
+        pe_mx1(0, (2, 3))
+        pe_tx(3)
+        pe_mx1(1)
+        pe_tx(4)
+        pe_tx(5)
+        pe_mx1(2)
+        pe_tx(6)
+        pe_tx(7)
+        for b in range(3, 6):
+            pe_mx1(b)
+        step("PE", "tb", ["cbrow"] + claim(XT_BANKS[0], "cb2"),
+             lambda: nc.tensor.transpose(out=bank_tile(("bt", 0), XT_BANKS[0], [P, P])[:], in_=browf[:], identity=ident[:]))
+        for b in range(6, NB):
+            pe_mx1(b)
+
+        step("DVE", "cb1", ["ld_b1"], lambda: nc.vector.tensor_copy(out=b1f[:], in_=b1raw[:]))
+        step("DVE", "rw1_0", ["ld_w1"], lambda: regroup_w1(0))
+        step("DVE", "rw1_1", ["ld_w1"], lambda: regroup_w1(1))
+        def v_xc(b, jj):
+            eng = "ACT" if (b, jj) in XC_ON_ACT else "DVE"
+            deps = ["tx%d" % b] + (["qx%d" % (b - XG_BUFS)] if b >= XG_BUFS else [])
+            step(eng, "xc%d_%d" % (b, jj), deps, lambda: xc(b, jj, eng))
+        def v_qx(b):
+            step("DVE", "qx%d" % b, ["xc%d_0" % b, "xc%d_1" % b], lambda: qx(b))
+        v_xc(0, 0)
+        v_xc(0, 1)
+        v_qx(0)
+        step("DVE", "qw1_0", ["rw1_0", "rw1_1"], lambda: quant_w("w1", 0, 256))
+        step("DVE", "rw1_2", ["ld_w1"], lambda: regroup_w1(2))
+        step("DVE", "rw1_3", ["ld_w1"], lambda: regroup_w1(3))
+        v_xc(1, 0)
+        step("DVE", "qw1_1", ["rw1_2", "rw1_3"], lambda: quant_w("w1", 256, 512))
+        v_xc(1, 1)
+        v_qx(1)
+        v_xc(2, 0)
+        v_xc(2, 1)
+        for b in range(3, NB):
+            v_xc(b, 0)
+            v_qx(b - 1)
+            v_xc(b, 1)
+        step("DVE", "rwv", ["ld_wv"], lambda: regroup_w("wv"))
+        v_qx(NB - 1)
+        step("DVE", "cbrow", ["ld_bias"], lambda: nc.vector.tensor_copy(out=browf[:], in_=brow[:]))
+        step("DVE", "rw2", ["ld_w2"], lambda: regroup_w("w2"))
+        step("DVE", "qwv", ["rwv"], lambda: quant_w("wv", 0, 512))
+        step("DVE", "qw2", ["rw2"], lambda: quant_w("w2", 0, 512))
+
+        def v_hr(b):
+            deps = ["silu%d_%d" % (b, t) for t in range(4)] + (["qh%d" % (b - HG_BUFS)] if b >= HG_BUFS else [])
+            step("DVE", "hr%d" % b, deps, lambda: hr(b))
+        def v_qh(b):
+            step("DVE", "qh%d" % b, ["hr%d" % b], lambda: qh(b))
+
+        for b in range(NB):
+            for t in range(4):
+                step("ACT", "silu%d_%d" % (b, t), ["mx1_%d_%d" % (b, t), "cb1", "warm"], lambda b=b, t=t: silu(b, t))
+
+        nbank = [0]
+        def next_bank(reader):
+            bank = nbank[0] % 8
+            nbank[0] += 1
+            return bank, claim(bank, reader)
+
+        def pe_mx2(b):
+            for c in range(4):
+                bank, war = next_bank("sg%d_%d" % (b, c))
+                step("PE", "g%d_%d" % (b, c), ["qh%d" % b, "qw2"] + war, lambda c=c, bank=bank: mx(("g", 4 * b + c), bank, "w2", c, hcod, hscl, b))
+                bank, war = next_bank("st%d_%d" % (b, c))
+                step("PE", "v%d_%d" % (b, c), ["qx%d" % b, "qwv"] + war, lambda c=c, bank=bank: mx(("v", 4 * b + c), bank, "wv", c, xcod, xscl, b))
+
+        def pe_tout(b):
+            for j in range(4):
+                bank, war = next_bank("ev%d_%d" % (b, j))
+                step("PE", "to%d_%d" % (b, j), ["st%d_%d" % (b, c) for c in range(4)] + war, lambda j=j, bank=bank: tout(b, j, bank))
+
+        pe_mx2(0)
+        for b in range(1, NB):
+            pe_mx2(b)
+            pe_tout(b - 1)
+        pe_tout(NB - 1)
+
+        def a_sg(b, c):
+            n = 4 * b + c
+            deps = ["g%d_%d" % (b, c), "cb2"] + (["st%d_%d" % ((n - SIG_BUFS) // 4, (n - SIG_BUFS) % 4)] if n >= SIG_BUFS else [])
+            step("ACT", "sg%d_%d" % (b, c), deps, lambda: sg(b, c))
+
+        def any_ev(b, j):
+            eng = "DVE" if (b, j) in EV_ON_DVE else "ACT"
+            deps = ["to%d_%d" % (b, j)] + (["store%d_%d" % (b - OSB_BUFS, j) for j in (1, 3)] if b >= OSB_BUFS else [])
+            step(eng, "ev%d_%d" % (b, j), deps, lambda: ev(b, j, eng))
+
+        def v_st(b, c):
+            deps = ["v%d_%d" % (b, c), "sg%d_%d" % (b, c)] + (["to%d_%d" % (b - OT_BUFS, j) for j in range(4)] if b >= OT_BUFS else [])
+            step("DVE", "st%d_%d" % (b, c), deps, lambda: st(b, c))
+
+        v_hr(0)
+        for b in range(1, H_EARLY):
+            v_hr(b)
+            v_qh(b - 1)
+            if b == 1:
+                step("DVE", "cb2", ["tb"], lambda: nc.vector.tensor_copy(out=b2v[:], in_=live[("bt", 0)][:, 0:8]))
+        v_qh(H_EARLY - 1)
+        def stores(b):
+            if b == NB - 1:
+                for j in range(4):
+                    step("SP", "store%d_%d" % (b, j), ["ev%d_%d" % (b, j)], lambda j=j: store(b, j, j + 1))
+            else:
+                for j in (0, 2):
+                    step("SP", "store%d_%d" % (b, j + 1), ["ev%d_%d" % (b, j), "ev%d_%d" % (b, j + 1)], lambda j=j: store(b, j, j + 2))
+
+        for b in range(NB + 1):
+            nxt = b + H_EARLY
+            if b < NB:
+                for c in range(4):
+                    a_sg(b, c)
+                    v_st(b, c)
+            if nxt < NB:
+                v_hr(nxt)
+            if b >= 1:
+                for j in range(4):
+                    any_ev(b - 1, j)
+            if nxt < NB:
+                v_qh(nxt)
+            if b >= 1:
+                stores(b - 1)
+
+        done = set()
+        heads = dict((e, 0) for e in order)
+        left = sum(len(v) for v in order.values())
+        while left:
+            moved = 0
+            for e in ("SP", "POOL", "PE", "DVE", "ACT"):
+                while heads[e] < len(order[e]):
+                    name = order[e][heads[e]]
+                    deps, fn = steps[name]
+                    if not all(d in done for d in deps):
+                        break
+                    fn()
+                    done.add(name)
+                    heads[e] += 1
+                    moved += 1
+            assert moved, "the orders wait for each other: %s" % [order[e][heads[e]] for e in order if heads[e] < len(order[e])]
+            left -= moved

@@ -16,19 +16,22 @@ PACK = 4
 DIM = 512
 TOKENS = 4096
 BLK = 512
+HALF = BLK // 2
 NB = TOKENS // BLK
 FLOPS = 3 * 2 * TOKENS * DIM * DIM
 
-XG_BUFS = 3
-HG_BUFS = 2
+UNITS1 = ((0, 0, HALF), (0, HALF, HALF)) + tuple((b, 0, BLK) for b in range(1, NB))
+UNITS2 = tuple((b, 0, BLK) for b in range(NB - 1)) + ((NB - 1, 0, HALF), (NB - 1, HALF, HALF))
+GRP_BUFS = 3
 SIG_BUFS = 4
 OT_BUFS = 2
 OSB_BUFS = 3
 XT_BANKS = (0, 1, 2, 3)
 Z_BANKS = (4, 5, 6, 7)
-XC_ON_ACT = ((0, 0), (0, 1), (1, 0), (1, 1))
-EV_ON_DVE = ((2, 3), (3, 1), (3, 3), (4, 1), (4, 3), (5, 1), (5, 3), (6, 1), (6, 3), (7, 1), (7, 3))
-H_EARLY = 5
+XC_ON_ACT = ((0, 0), (0, 1))
+EV_ON_DVE = ((3, 1), (3, 3), (4, 1), (4, 3), (5, 1), (5, 3), (6, 1), (6, 3), (7, 1), (7, 3))
+H_EARLY = 4
+HR_ON_POOL = ()
 
 
 def tile_selectivemixing_pa_t_kernel(tc, x, W1, b1, W2g, b2g, Wv, bv, out):
@@ -39,6 +42,7 @@ def tile_selectivemixing_pa_t_kernel(tc, x, W1, b1, W2g, b2g, Wv, bv, out):
     order = {"SP": [], "POOL": [], "PE": [], "DVE": [], "ACT": []}
 
     def step(engine, name, deps, fn):
+        assert name not in steps, name
         steps[name] = (deps, fn)
         order[engine].append(name)
 
@@ -88,11 +92,25 @@ def tile_selectivemixing_pa_t_kernel(tc, x, W1, b1, W2g, b2g, Wv, bv, out):
             last_reader[bank] = reader
             return [prev] if prev else []
 
-        cols = lambda b: slice(b * BLK, (b + 1) * BLK)
+        def grp_slot(n):
+            first_pool = NB + min(HR_ON_POOL) if HR_ON_POOL else 2 * NB
+            return (min(n, first_pool - 1)) % GRP_BUFS
 
-        def ld_x(b):
+        def grp_prev(n):
+            mine = grp_slot(n)
+            for m in range(n - 1, -1, -1):
+                if grp_slot(m) == mine:
+                    return ["qh%d" % (m - NB) if m >= NB else "qx%d" % (m + 1)]
+            return []
+
+        def cols(unit):
+            b, c0, n = unit
+            return slice(b * BLK + c0, b * BLK + c0 + n)
+
+        def ld_x(b, j0, j1):
             nc.sync.dma_start(
-                out=xsb[b][:].rearrange("p (j d) -> p j d", j=PACK), in_=xf[cols(b), :].rearrange("(p j) d -> p j d", j=PACK)
+                out=xsb[b][:].rearrange("p (j d) -> p j d", j=PACK)[:, j0:j1, :],
+                in_=xf[b * BLK:(b + 1) * BLK, :].rearrange("(p j) d -> p j d", j=PACK)[:, j0:j1, :],
             )
 
         def ld_w_pairs(w, src):
@@ -107,12 +125,6 @@ def tile_selectivemixing_pa_t_kernel(tc, x, W1, b1, W2g, b2g, Wv, bv, out):
         def memsets():
             nc.vector.memset(warm[:], 0.0)
             nc.vector.memset(brow[:], 0.0)
-
-        def warm_table():
-            nc.scalar.activation(out=warm[:, 1:2], in_=warm[:, 0:1], func=ACT.Silu)
-
-        def ld_b1():
-            nc.sync.dma_start(out=b1raw[:], in_=b1.rearrange("(p t) -> p t", t=PACK))
 
         def ld_bias():
             nc.sync.dma_start(out=brow[0:4, :], in_=b2g.rearrange("(c p) -> c p", p=P))
@@ -135,17 +147,16 @@ def tile_selectivemixing_pa_t_kernel(tc, x, W1, b1, W2g, b2g, Wv, bv, out):
                 out=wcod[w][:, lo:hi].bitcast(FP8X4), scales=wscl[w][:, lo:hi], in_=wgrp[w][:, lo * PACK:hi * PACK]
             )
 
-        def tx(b):
+        def tx(b, jj):
             words = xsb[b][:].bitcast(F32)
-            for jj in range(2):
-                xt = bank_tile(("xt", 2 * b + jj), XT_BANKS[(2 * b + jj) % len(XT_BANKS)], [P, 2, 2 * P])
-                for jl in range(2):
-                    for u in range(2):
-                        w0 = ((2 * jj + jl) * 2 + u) * P
-                        nc.tensor.transpose(out=xt[:, u, jl * P:(jl + 1) * P], in_=words[:, w0:w0 + P], identity=ident[:])
+            xt = bank_tile(("xt", 2 * b + jj), XT_BANKS[(2 * b + jj) % len(XT_BANKS)], [P, 2, HALF])
+            for jl in range(2):
+                for u in range(2):
+                    w0 = ((2 * jj + jl) * 2 + u) * P
+                    nc.tensor.transpose(out=xt[:, u, jl * P:(jl + 1) * P], in_=words[:, w0:w0 + P], identity=ident[:])
 
         def xc(b, jj, engine):
-            xg = ring_tile(("xg", b), [P, BLK * PACK], BF16, "xg", XG_BUFS, 64)
+            xg = ring_tile(("xg", b), [P, BLK * PACK], BF16, "grp%d" % grp_slot(b), 1, 64)
             dst = xg[:].bitcast(F32)[:, jj * BLK:(jj + 1) * BLK].rearrange("p (c u) -> p c u", u=2)
             src = live[("xt", 2 * b + jj)][:].rearrange("p u c -> p c u")
             if engine == "ACT":
@@ -153,42 +164,52 @@ def tile_selectivemixing_pa_t_kernel(tc, x, W1, b1, W2g, b2g, Wv, bv, out):
             else:
                 nc.vector.tensor_copy(out=dst, in_=src)
 
-        def qx(b):
-            nc.vector.quantize_mx(out=xcod[:, cols(b)].bitcast(FP8X4), scales=xscl[:, cols(b)], in_=live[("xg", b)][:])
+        def qx(unit):
+            b, c0, n = unit
+            nc.vector.quantize_mx(
+                out=xcod[:, cols(unit)].bitcast(FP8X4), scales=xscl[:, cols(unit)],
+                in_=live[("xg", b)][:, c0 * PACK:(c0 + n) * PACK],
+            )
 
-        def mx(key, bank, w, c, cod, scl, b):
-            acc = bank_tile(key, bank, [P, BLK])
+        def mx(key, bank, w, c, cod, scl, unit):
+            acc = bank_tile(key, bank, [P, unit[2]])
             nc.tensor.matmul_mx(
                 out=acc[:],
                 lhsT=wcod[w][:, c * P:(c + 1) * P].bitcast(FP8X4),
                 lhsT_scale=wscl[w][:, c * P:(c + 1) * P],
-                rhs=cod[:, cols(b)].bitcast(FP8X4),
-                rhs_scale=scl[:, cols(b)],
+                rhs=cod[:, cols(unit)].bitcast(FP8X4),
+                rhs_scale=scl[:, cols(unit)],
                 start=True,
                 stop=True,
             )
 
-        def silu(b, t):
-            nc.scalar.activation(out=hraw[b][:, t, :], in_=live[("z", 4 * b + t)][:], func=ACT.Silu, bias=b1f[:, t:t + 1])
+        def silu(i, t):
+            b, c0, n = UNITS1[i]
+            nc.scalar.activation(out=hraw[b][:, t, c0:c0 + n], in_=live[("z", 4 * i + t)][:], func=ACT.Silu, bias=b1f[:, t:t + 1])
 
-        def hr(b):
-            hg = ring_tile(("hg", b), [P, BLK * PACK], BF16, "hg", HG_BUFS, 64)
-            nc.vector.tensor_copy(
-                out=hg[:].rearrange("p (c i k) -> p c k i", i=4, k=PACK),
-                in_=hraw[b][:].rearrange("p k (c i) -> p c k i", i=4),
-            )
+        def hr(b, engine):
+            hg = ring_tile(("hg", b), [P, BLK * PACK], BF16, "grp%d" % grp_slot(NB + b), 1, 64)
+            dst = hg[:].rearrange("p (c i k) -> p c k i", i=4, k=PACK)
+            src = hraw[b][:].rearrange("p k (c i) -> p c k i", i=4)
+            if engine == "POOL":
+                nc.gpsimd.tensor_scalar(out=dst, in0=src, scalar1=1.0, scalar2=0.0, op0=ALU.mult, op1=ALU.add)
+            else:
+                nc.vector.tensor_copy(out=dst, in_=src)
 
         def qh(b):
-            nc.vector.quantize_mx(out=hcod[:, cols(b)].bitcast(FP8X4), scales=hscl[:, cols(b)], in_=live[("hg", b)][:])
+            nc.vector.quantize_mx(
+                out=hcod[:, b * BLK:(b + 1) * BLK].bitcast(FP8X4), scales=hscl[:, b * BLK:(b + 1) * BLK], in_=live[("hg", b)][:]
+            )
 
-        def sg(b, c):
-            s = ring_tile(("sig", 4 * b + c), [P, BLK], F32, "sig", SIG_BUFS)
-            nc.scalar.activation(out=s[:], in_=live[("g", 4 * b + c)][:], func=ACT.Sigmoid, bias=b2v[:, c:c + 1])
+        def sg(i, c):
+            s = ring_tile(("sig", 4 * i + c), [P, UNITS2[i][2]], F32, "sig", SIG_BUFS)
+            nc.scalar.activation(out=s[:], in_=live[("g", 4 * i + c)][:], func=ACT.Sigmoid, bias=b2v[:, c:c + 1])
 
-        def st(b, c):
+        def st(i, c):
+            b, c0, n = UNITS2[i]
             o = ring_tile(("ot", b), [P, PACK, BLK], F32, "ot", OT_BUFS)
             nc.vector.scalar_tensor_tensor(
-                out=o[:, c, :], in0=live[("v", 4 * b + c)][:], scalar=b2v[:, 4 + c:5 + c], in1=live[("sig", 4 * b + c)][:],
+                out=o[:, c, c0:c0 + n], in0=live[("v", 4 * i + c)][:], scalar=b2v[:, 4 + c:5 + c], in1=live[("sig", 4 * i + c)][:],
                 op0=ALU.add, op1=ALU.mult,
             )
 
@@ -206,132 +227,167 @@ def tile_selectivemixing_pa_t_kernel(tc, x, W1, b1, W2g, b2g, Wv, bv, out):
 
         def store(b, j0, j1):
             nc.sync.dma_start(
-                out=of[cols(b), :].rearrange("(p j) d -> p j d", j=PACK)[:, j0:j1, :], in_=live[("osb", b)][:, j0:j1, :]
+                out=of[b * BLK:(b + 1) * BLK, :].rearrange("(p j) d -> p j d", j=PACK)[:, j0:j1, :], in_=live[("osb", b)][:, j0:j1, :]
             )
 
         step("POOL", "ident", [], lambda: make_identity(nc, ident[:]))
-        step("SP", "ld_b1", [], ld_b1)
-        step("SP", "ld_x0", [], lambda: ld_x(0))
+        step("SP", "ld_b1", [], lambda: nc.sync.dma_start(out=b1raw[:], in_=b1.rearrange("(p t) -> p t", t=PACK)))
+        step("SP", "ld_x0_0", [], lambda: ld_x(0, 0, 2))
         step("SP", "ld_w1", [], lambda: ld_w_pairs("w1", W1))
+        step("SP", "ld_x0_1", [], lambda: ld_x(0, 2, 4))
         for b in range(1, NB):
-            step("SP", "ld_x%d" % b, [], lambda b=b: ld_x(b))
+            step("SP", "ld_x%d" % b, [], lambda b=b: ld_x(b, 0, 4))
         step("SP", "ld_wv", [], lambda: ld_w_pairs("wv", Wv))
         step("SP", "ld_w2", [], lambda: ld_w_rows("w2", W2g))
         step("SP", "ld_bias", ["memsets"], ld_bias)
 
         step("DVE", "memsets", [], memsets)
-        step("ACT", "warm", ["memsets"], warm_table)
+        step("ACT", "warm", ["memsets"], lambda: nc.scalar.activation(out=warm[:, 1:2], in_=warm[:, 0:1], func=ACT.Silu))
 
-        def pe_tx(b):
-            deps = ["ld_x%d" % b, "ident"]
-            for jj in range(2):
+        def pe_tx(b, jjs=(0, 1)):
+            for jj in jjs:
+                deps = ["ld_x0_%d" % jj if b == 0 else "ld_x%d" % b, "ident"]
                 deps += claim(XT_BANKS[(2 * b + jj) % len(XT_BANKS)], "xc%d_%d" % (b, jj))
-            step("PE", "tx%d" % b, deps, lambda: tx(b))
+                step("PE", "tx%d_%d" % (b, jj), deps, lambda jj=jj: tx(b, jj))
 
-        def pe_mx1(b, ts=(0, 1, 2, 3)):
+        def pe_mx1(i, ts=(0, 1, 2, 3)):
             for t in ts:
-                bank = Z_BANKS[(4 * b + t) % len(Z_BANKS)]
-                deps = ["qx%d" % b, "qw1_%d" % (t // 2)] + claim(bank, "silu%d_%d" % (b, t))
-                step("PE", "mx1_%d_%d" % (b, t), deps, lambda t=t, bank=bank: mx(("z", 4 * b + t), bank, "w1", t, xcod, xscl, b))
+                bank = Z_BANKS[(4 * i + t) % len(Z_BANKS)]
+                deps = ["qx%d" % i, "qw1_%d" % t] + claim(bank, "silu%d_%d" % (i, t))
+                step("PE", "mx1_%d_%d" % (i, t), deps, lambda t=t, bank=bank: mx(("z", 4 * i + t), bank, "w1", t, xcod, xscl, UNITS1[i]))
 
         pe_tx(0)
-        pe_tx(1)
         pe_mx1(0, (0, 1))
-        pe_tx(2)
+        pe_tx(1)
         pe_mx1(0, (2, 3))
-        pe_tx(3)
         pe_mx1(1)
-        pe_tx(4)
-        pe_tx(5)
+        pe_tx(2)
+        pe_tx(3)
         pe_mx1(2)
+        pe_tx(4)
+        pe_mx1(3)
+        pe_tx(5)
         pe_tx(6)
+        pe_mx1(4)
         pe_tx(7)
-        for b in range(3, 6):
-            pe_mx1(b)
+        pe_mx1(5)
+        pe_mx1(6)
         step("PE", "tb", ["cbrow"] + claim(XT_BANKS[0], "cb2"),
              lambda: nc.tensor.transpose(out=bank_tile(("bt", 0), XT_BANKS[0], [P, P])[:], in_=browf[:], identity=ident[:]))
-        for b in range(6, NB):
-            pe_mx1(b)
+        pe_mx1(7)
+        pe_mx1(8)
 
-        step("DVE", "cb1", ["ld_b1"], lambda: nc.vector.tensor_copy(out=b1f[:], in_=b1raw[:]))
-        step("DVE", "rw1_0", ["ld_w1"], lambda: regroup_w1(0))
-        step("DVE", "rw1_1", ["ld_w1"], lambda: regroup_w1(1))
         def v_xc(b, jj):
             eng = "ACT" if (b, jj) in XC_ON_ACT else "DVE"
-            deps = ["tx%d" % b] + (["qx%d" % (b - XG_BUFS)] if b >= XG_BUFS else [])
+            deps = ["tx%d_%d" % (b, jj)] + grp_prev(b)
             step(eng, "xc%d_%d" % (b, jj), deps, lambda: xc(b, jj, eng))
-        def v_qx(b):
-            step("DVE", "qx%d" % b, ["xc%d_0" % b, "xc%d_1" % b], lambda: qx(b))
+
+        def v_qx(i):
+            b, c0, n = UNITS1[i]
+            step("DVE", "qx%d" % i, ["xc%d_%d" % (b, jj) for jj in range(c0 // HALF, (c0 + n) // HALF)], lambda: qx(UNITS1[i]))
+
+        def v_rw1(t):
+            step("DVE", "rw1_%d" % t, ["ld_w1"], lambda: regroup_w1(t))
+
+        def v_qw1(t):
+            step("DVE", "qw1_%d" % t, ["rw1_%d" % t], lambda: quant_w("w1", t * P, (t + 1) * P))
+
+        step("DVE", "cb1", ["ld_b1"], lambda: nc.vector.tensor_copy(out=b1f[:], in_=b1raw[:]))
         v_xc(0, 0)
         v_xc(0, 1)
+        v_rw1(0)
+        v_rw1(1)
+        v_qw1(0)
         v_qx(0)
-        step("DVE", "qw1_0", ["rw1_0", "rw1_1"], lambda: quant_w("w1", 0, 256))
-        step("DVE", "rw1_2", ["ld_w1"], lambda: regroup_w1(2))
-        step("DVE", "rw1_3", ["ld_w1"], lambda: regroup_w1(3))
-        v_xc(1, 0)
-        step("DVE", "qw1_1", ["rw1_2", "rw1_3"], lambda: quant_w("w1", 256, 512))
-        v_xc(1, 1)
+        v_rw1(2)
+        v_qw1(1)
+        v_rw1(3)
+        v_qw1(2)
         v_qx(1)
+        v_qw1(3)
+        v_xc(1, 0)
+        v_xc(1, 1)
+        v_qx(2)
         v_xc(2, 0)
         v_xc(2, 1)
         for b in range(3, NB):
             v_xc(b, 0)
-            v_qx(b - 1)
+            v_qx(b)
             v_xc(b, 1)
         step("DVE", "rwv", ["ld_wv"], lambda: regroup_w("wv"))
-        v_qx(NB - 1)
+        v_qx(NB)
         step("DVE", "cbrow", ["ld_bias"], lambda: nc.vector.tensor_copy(out=browf[:], in_=brow[:]))
         step("DVE", "rw2", ["ld_w2"], lambda: regroup_w("w2"))
-        step("DVE", "qwv", ["rwv"], lambda: quant_w("wv", 0, 512))
-        step("DVE", "qw2", ["rw2"], lambda: quant_w("w2", 0, 512))
+        step("DVE", "qwv", ["rwv"], lambda: quant_w("wv", 0, DIM))
+        step("DVE", "qw2", ["rw2"], lambda: quant_w("w2", 0, DIM))
 
         def v_hr(b):
-            deps = ["silu%d_%d" % (b, t) for t in range(4)] + (["qh%d" % (b - HG_BUFS)] if b >= HG_BUFS else [])
-            step("DVE", "hr%d" % b, deps, lambda: hr(b))
+            eng = "POOL" if b in HR_ON_POOL else "DVE"
+            deps = ["silu%d_%d" % (i, t) for i in range(len(UNITS1)) if UNITS1[i][0] == b for t in range(4)] + grp_prev(NB + b)
+            step(eng, "hr%d" % b, deps, lambda: hr(b, eng))
+
         def v_qh(b):
             step("DVE", "qh%d" % b, ["hr%d" % b], lambda: qh(b))
 
-        for b in range(NB):
+        for i in range(len(UNITS1)):
             for t in range(4):
-                step("ACT", "silu%d_%d" % (b, t), ["mx1_%d_%d" % (b, t), "cb1", "warm"], lambda b=b, t=t: silu(b, t))
+                step("ACT", "silu%d_%d" % (i, t), ["mx1_%d_%d" % (i, t), "cb1", "warm"], lambda i=i, t=t: silu(i, t))
 
         nbank = [0]
+
         def next_bank(reader):
             bank = nbank[0] % 8
             nbank[0] += 1
             return bank, claim(bank, reader)
 
-        def pe_mx2(b):
-            for c in range(4):
-                bank, war = next_bank("sg%d_%d" % (b, c))
-                step("PE", "g%d_%d" % (b, c), ["qh%d" % b, "qw2"] + war, lambda c=c, bank=bank: mx(("g", 4 * b + c), bank, "w2", c, hcod, hscl, b))
-                bank, war = next_bank("st%d_%d" % (b, c))
-                step("PE", "v%d_%d" % (b, c), ["qx%d" % b, "qwv"] + war, lambda c=c, bank=bank: mx(("v", 4 * b + c), bank, "wv", c, xcod, xscl, b))
+        def js_of(i):
+            b, c0, n = UNITS2[i]
+            return [(b, j) for j in range(c0 // P, (c0 + n) // P)]
 
-        def pe_tout(b):
-            for j in range(4):
+        def pe_mx2(i):
+            b = UNITS2[i][0]
+            for c in range(4):
+                bank, war = next_bank("sg%d_%d" % (i, c))
+                step("PE", "g%d_%d" % (i, c), ["qh%d" % b, "qw2"] + war, lambda c=c, bank=bank: mx(("g", 4 * i + c), bank, "w2", c, hcod, hscl, UNITS2[i]))
+                bank, war = next_bank("st%d_%d" % (i, c))
+                step("PE", "v%d_%d" % (i, c), ["qx%d" % (b + 1), "qwv"] + war, lambda c=c, bank=bank: mx(("v", 4 * i + c), bank, "wv", c, xcod, xscl, UNITS2[i]))
+
+        def pe_tout(i):
+            for b, j in js_of(i):
                 bank, war = next_bank("ev%d_%d" % (b, j))
-                step("PE", "to%d_%d" % (b, j), ["st%d_%d" % (b, c) for c in range(4)] + war, lambda j=j, bank=bank: tout(b, j, bank))
+                step("PE", "to%d_%d" % (b, j), ["st%d_%d" % (i, c) for c in range(4)] + war, lambda b=b, j=j, bank=bank: tout(b, j, bank))
 
         pe_mx2(0)
-        for b in range(1, NB):
-            pe_mx2(b)
-            pe_tout(b - 1)
-        pe_tout(NB - 1)
+        for i in range(1, len(UNITS2)):
+            pe_mx2(i)
+            pe_tout(i - 1)
+        pe_tout(len(UNITS2) - 1)
 
-        def a_sg(b, c):
-            n = 4 * b + c
-            deps = ["g%d_%d" % (b, c), "cb2"] + (["st%d_%d" % ((n - SIG_BUFS) // 4, (n - SIG_BUFS) % 4)] if n >= SIG_BUFS else [])
-            step("ACT", "sg%d_%d" % (b, c), deps, lambda: sg(b, c))
+        def a_sg(i, c):
+            n = 4 * i + c - SIG_BUFS
+            deps = ["g%d_%d" % (i, c), "cb2"] + (["st%d_%d" % (n // 4, n % 4)] if n >= 0 else [])
+            step("ACT", "sg%d_%d" % (i, c), deps, lambda: sg(i, c))
+
+        store_names = dict((b, []) for b in range(NB))
 
         def any_ev(b, j):
             eng = "DVE" if (b, j) in EV_ON_DVE else "ACT"
-            deps = ["to%d_%d" % (b, j)] + (["store%d_%d" % (b - OSB_BUFS, j) for j in (1, 3)] if b >= OSB_BUFS else [])
+            deps = ["to%d_%d" % (b, j)] + (store_names[b - OSB_BUFS] if b >= OSB_BUFS else [])
             step(eng, "ev%d_%d" % (b, j), deps, lambda: ev(b, j, eng))
 
-        def v_st(b, c):
-            deps = ["v%d_%d" % (b, c), "sg%d_%d" % (b, c)] + (["to%d_%d" % (b - OT_BUFS, j) for j in range(4)] if b >= OT_BUFS else [])
-            step("DVE", "st%d_%d" % (b, c), deps, lambda: st(b, c))
+        def v_st(i, c):
+            b = UNITS2[i][0]
+            deps = ["v%d_%d" % (i, c), "sg%d_%d" % (i, c)] + (["to%d_%d" % (b - OT_BUFS, j) for j in range(4)] if b >= OT_BUFS else [])
+            step("DVE", "st%d_%d" % (i, c), deps, lambda: st(i, c))
+
+        def stores(i):
+            js = js_of(i)
+            width = 1 if i == len(UNITS2) - 1 else 2
+            for k in range(0, len(js), width):
+                b, j = js[k]
+                name = "store%d_%d" % (b, j)
+                store_names[b].append(name)
+                step("SP", name, ["ev%d_%d" % (b, j + d) for d in range(width)], lambda b=b, j=j: store(b, j, j + width))
 
         v_hr(0)
         for b in range(1, H_EARLY):
@@ -340,29 +396,21 @@ def tile_selectivemixing_pa_t_kernel(tc, x, W1, b1, W2g, b2g, Wv, bv, out):
             if b == 1:
                 step("DVE", "cb2", ["tb"], lambda: nc.vector.tensor_copy(out=b2v[:], in_=live[("bt", 0)][:, 0:8]))
         v_qh(H_EARLY - 1)
-        def stores(b):
-            if b == NB - 1:
-                for j in range(4):
-                    step("SP", "store%d_%d" % (b, j), ["ev%d_%d" % (b, j)], lambda j=j: store(b, j, j + 1))
-            else:
-                for j in (0, 2):
-                    step("SP", "store%d_%d" % (b, j + 1), ["ev%d_%d" % (b, j), "ev%d_%d" % (b, j + 1)], lambda j=j: store(b, j, j + 2))
-
-        for b in range(NB + 1):
-            nxt = b + H_EARLY
-            if b < NB:
+        for i in range(len(UNITS2) + 1):
+            nxt = i + H_EARLY
+            if i < len(UNITS2):
                 for c in range(4):
-                    a_sg(b, c)
-                    v_st(b, c)
+                    a_sg(i, c)
+                    v_st(i, c)
             if nxt < NB:
                 v_hr(nxt)
-            if b >= 1:
-                for j in range(4):
-                    any_ev(b - 1, j)
+            if i >= 1:
+                for b, j in js_of(i - 1):
+                    any_ev(b, j)
             if nxt < NB:
                 v_qh(nxt)
-            if b >= 1:
-                stores(b - 1)
+            if i >= 1:
+                stores(i - 1)
 
         done = set()
         heads = dict((e, 0) for e in order)

@@ -29,9 +29,9 @@ OSB_BUFS = 3
 XT_BANKS = (0, 1, 2, 3)
 Z_BANKS = (4, 5, 6, 7)
 XC_ON_ACT = ((0, 0), (0, 1))
-EV_ON_DVE = ((3, 1), (3, 3), (4, 1), (4, 3), (5, 1), (5, 3), (6, 1), (6, 3), (7, 1), (7, 3))
+EV_ON_DVE = ((0, 3), (1, 3), (2, 3), (3, 1), (3, 3), (4, 1), (4, 3), (5, 1), (5, 3), (6, 1), (6, 3), (7, 1), (7, 3))
 H_EARLY = 4
-HR_ON_POOL = ()
+HR_ON_POOL = (4, 5, 6, 7)
 
 
 def tile_selectivemixing_pa_t_kernel(tc, x, W1, b1, W2g, b2g, Wv, bv, out):

@@ -29,9 +29,9 @@ OSB_BUFS = 3
 XT_BANKS = (0, 1, 2, 3)
 Z_BANKS = (4, 5, 6, 7)
 XC_ON_ACT = ((0, 0), (0, 1))
-EV_ON_DVE = ((0, 3), (1, 3), (2, 3), (3, 1), (3, 3), (4, 1), (4, 3), (5, 1), (5, 3), (6, 1), (6, 3), (7, 1), (7, 3))
-H_EARLY = 4
-HR_ON_POOL = (4, 5, 6, 7)
+EV_ON_DVE = ((0, 3), (1, 3), (2, 3), (3, 3), (4, 1), (4, 3), (5, 1), (5, 3), (6, 1), (6, 3), (7, 1), (7, 3))
+H_EARLY = 3
+HR_ON_POOL = (3, 4, 5, 6, 7)
 
 
 def tile_selectivemixing_pa_t_kernel(tc, x, W1, b1, W2g, b2g, Wv, bv, out):

from contextlib import ExitStack

import concourse.mybir as mybir
from concourse.masks import make_identity

F32 = mybir.dt.float32
BF16 = mybir.dt.bfloat16
U32 = mybir.dt.uint32
U8 = mybir.dt.uint8
FP8X4 = mybir.dt.float8_e4m3fn_x4
ACT = mybir.ActivationFunctionType
ALU = mybir.AluOpType

P = 128
PACK = 4
DIM = 512
TOKENS = 4096
BLK = 512
HALF = BLK // 2
NB = TOKENS // BLK
FLOPS = 3 * 2 * TOKENS * DIM * DIM

UNITS1 = ((0, 0, HALF), (0, HALF, HALF)) + tuple((b, 0, BLK) for b in range(1, NB))
UNITS2 = tuple((b, 0, BLK) for b in range(NB - 1)) + ((NB - 1, 0, HALF), (NB - 1, HALF, HALF))
GRP_BUFS = 3
SIG_BUFS = 4
OT_BUFS = 2
OSB_BUFS = 3
XT_BANKS = (0, 1, 2, 3)
Z_BANKS = (4, 5, 6, 7)
XC_ON_ACT = ((0, 0), (0, 1))
EV_ON_DVE = ((0, 3), (1, 3), (2, 3), (3, 3), (4, 1), (4, 3), (5, 1), (5, 3), (6, 1), (6, 3), (7, 1), (7, 3))
H_EARLY = 3
HR_ON_POOL = (3, 4, 5, 6, 7)


def tile_selectivemixing_pa_t_kernel(tc, x, W1, b1, W2g, b2g, Wv, bv, out):
    nc = tc.nc
    xf = x.flatten_outer_dims()
    of = out.flatten_outer_dims()
    steps = {}
    order = {"SP": [], "POOL": [], "PE": [], "DVE": [], "ACT": []}

    def step(engine, name, deps, fn):
        assert name not in steps, name
        steps[name] = (deps, fn)
        order[engine].append(name)

    with ExitStack() as ctx:
        keep = ctx.enter_context(tc.tile_pool(name="keep", bufs=1))
        ring = ctx.enter_context(tc.tile_pool(name="ring", bufs=1))
        psum = ctx.enter_context(tc.psum_pool(name="psum", bufs=1))
        ctx.enter_context(tc.manual_schedule())

        ident = keep.tile([P, P], F32, name="ident")
        warm = keep.tile([P, 2], F32, name="warm")
        b1raw = keep.tile([P, PACK], BF16, name="b1raw")
        b1f = keep.tile([P, PACK], F32, name="b1f")
        brow = keep.tile([P, P], BF16, name="brow")
        browf = keep.tile([P, P], F32, name="browf")
        b2v = keep.tile([P, 8], F32, name="b2v")
        wraw = {}
        wgrp = {}
        wcod = {}
        wscl = {}
        for w in ("w1", "wv", "w2"):
            wraw[w] = keep.tile([P, PACK, DIM], BF16, name=w + "raw")
            wgrp[w] = keep.tile([P, DIM * PACK], BF16, name=w + "grp", align_bytes=64)
            wcod[w] = keep.tile([P, DIM], U32, name=w + "cod", align_bytes=64)
            wscl[w] = keep.tile([P, DIM], U8, name=w + "scl", align_bytes=64)
        xcod = keep.tile([P, TOKENS], U32, name="xcod", align_bytes=64)
        xscl = keep.tile([P, TOKENS], U8, name="xscl", align_bytes=64)
        hcod = keep.tile([P, TOKENS], U32, name="hcod", align_bytes=64)
        hscl = keep.tile([P, TOKENS], U8, name="hscl", align_bytes=64)
        xsb = [keep.tile([P, PACK * DIM], BF16, name="xsb%d" % b) for b in range(NB)]
        hraw = [keep.tile([P, PACK, BLK], BF16, name="hraw%d" % b) for b in range(NB)]
        live = {}

        def ring_tile(key, shape, dtype, tag, bufs, align=None):
            if key not in live:
                live[key] = ring.tile(shape, dtype, name="%s_%s" % key, tag=tag, bufs=bufs, align_bytes=align)
            return live[key]

        def bank_tile(key, bank, shape):
            live[key] = psum.tile(shape, F32, name="ps_%s_%s" % key, tag="bank%d" % bank)
            return live[key]

        last_reader = {}

        def claim(bank, reader):
            prev = last_reader.get(bank)
            last_reader[bank] = reader
            return [prev] if prev else []

        def grp_slot(n):
            first_pool = NB + min(HR_ON_POOL) if HR_ON_POOL else 2 * NB
            return (min(n, first_pool - 1)) % GRP_BUFS

        def grp_prev(n):
            mine = grp_slot(n)
            for m in range(n - 1, -1, -1):
                if grp_slot(m) == mine:
                    return ["qh%d" % (m - NB) if m >= NB else "qx%d" % (m + 1)]
            return []

        def cols(unit):
            b, c0, n = unit
            return slice(b * BLK + c0, b * BLK + c0 + n)

        def ld_x(b, j0, j1):
            nc.sync.dma_start(
                out=xsb[b][:].rearrange("p (j d) -> p j d", j=PACK)[:, j0:j1, :],
                in_=xf[b * BLK:(b + 1) * BLK, :].rearrange("(p j) d -> p j d", j=PACK)[:, j0:j1, :],
            )

        def ld_w_pairs(w, src):
            nc.sync.dma_start(
                out=wraw[w][:].rearrange("q (u e) c -> q u (e c)", u=2),
                in_=src.rearrange("(u q e) c -> q u (e c)", u=2, e=2),
            )

        def ld_w_rows(w, src):
            nc.sync.dma_start(out=wraw[w][:], in_=src.rearrange("(p j) c -> p j c", j=PACK))

        def memsets():
            nc.vector.memset(warm[:], 0.0)
            nc.vector.memset(brow[:], 0.0)

        def ld_bias():
            nc.sync.dma_start(out=brow[0:4, :], in_=b2g.rearrange("(c p) -> c p", p=P))
            nc.sync.dma_start(out=brow[4:8, :], in_=bv.rearrange("(c p) -> c p", p=P))

        def regroup_w1(t):
            nc.vector.tensor_copy(
                out=wgrp["w1"][:, t * BLK:(t + 1) * BLK].rearrange("p (m k) -> p m k", k=PACK),
                in_=wraw["w1"][:].rearrange("p k (m t) -> p t m k", t=PACK)[:, t],
            )

        def regroup_w(w):
            nc.vector.tensor_copy(
                out=wgrp[w][:].rearrange("p (c i k) -> p c k i", i=4, k=PACK),
                in_=wraw[w][:].rearrange("p k (c i) -> p c k i", i=4),
            )

        def quant_w(w, lo, hi):
            nc.vector.quantize_mx(
                out=wcod[w][:, lo:hi].bitcast(FP8X4), scales=wscl[w][:, lo:hi], in_=wgrp[w][:, lo * PACK:hi * PACK]
            )

        def tx(b, jj):
            words = xsb[b][:].bitcast(F32)
            xt = bank_tile(("xt", 2 * b + jj), XT_BANKS[(2 * b + jj) % len(XT_BANKS)], [P, 2, HALF])
            for jl in range(2):
                for u in range(2):
                    w0 = ((2 * jj + jl) * 2 + u) * P
                    nc.tensor.transpose(out=xt[:, u, jl * P:(jl + 1) * P], in_=words[:, w0:w0 + P], identity=ident[:])

        def xc(b, jj, engine):
            xg = ring_tile(("xg", b), [P, BLK * PACK], BF16, "grp%d" % grp_slot(b), 1, 64)
            dst = xg[:].bitcast(F32)[:, jj * BLK:(jj + 1) * BLK].rearrange("p (c u) -> p c u", u=2)
            src = live[("xt", 2 * b + jj)][:].rearrange("p u c -> p c u")
            if engine == "ACT":
                nc.scalar.copy(out=dst, in_=src)
            else:
                nc.vector.tensor_copy(out=dst, in_=src)

        def qx(unit):
            b, c0, n = unit
            nc.vector.quantize_mx(
                out=xcod[:, cols(unit)].bitcast(FP8X4), scales=xscl[:, cols(unit)],
                in_=live[("xg", b)][:, c0 * PACK:(c0 + n) * PACK],
            )

        def mx(key, bank, w, c, cod, scl, unit):
            acc = bank_tile(key, bank, [P, unit[2]])
            nc.tensor.matmul_mx(
                out=acc[:],
                lhsT=wcod[w][:, c * P:(c + 1) * P].bitcast(FP8X4),
                lhsT_scale=wscl[w][:, c * P:(c + 1) * P],
                rhs=cod[:, cols(unit)].bitcast(FP8X4),
                rhs_scale=scl[:, cols(unit)],
                start=True,
                stop=True,
            )

        def silu(i, t):
            b, c0, n = UNITS1[i]
            nc.scalar.activation(out=hraw[b][:, t, c0:c0 + n], in_=live[("z", 4 * i + t)][:], func=ACT.Silu, bias=b1f[:, t:t + 1])

        def hr(b, engine):
            hg = ring_tile(("hg", b), [P, BLK * PACK], BF16, "grp%d" % grp_slot(NB + b), 1, 64)
            dst = hg[:].rearrange("p (c i k) -> p c k i", i=4, k=PACK)
            src = hraw[b][:].rearrange("p k (c i) -> p c k i", i=4)
            if engine == "POOL":
                nc.gpsimd.tensor_scalar(out=dst, in0=src, scalar1=1.0, scalar2=0.0, op0=ALU.mult, op1=ALU.add)
            else:
                nc.vector.tensor_copy(out=dst, in_=src)

        def qh(b):
            nc.vector.quantize_mx(
                out=hcod[:, b * BLK:(b + 1) * BLK].bitcast(FP8X4), scales=hscl[:, b * BLK:(b + 1) * BLK], in_=live[("hg", b)][:]
            )

        def sg(i, c):
            s = ring_tile(("sig", 4 * i + c), [P, UNITS2[i][2]], F32, "sig", SIG_BUFS)
            nc.scalar.activation(out=s[:], in_=live[("g", 4 * i + c)][:], func=ACT.Sigmoid, bias=b2v[:, c:c + 1])

        def st(i, c):
            b, c0, n = UNITS2[i]
            o = ring_tile(("ot", b), [P, PACK, BLK], F32, "ot", OT_BUFS)
            nc.vector.scalar_tensor_tensor(
                out=o[:, c, c0:c0 + n], in0=live[("v", 4 * i + c)][:], scalar=b2v[:, 4 + c:5 + c], in1=live[("sig", 4 * i + c)][:],
                op0=ALU.add, op1=ALU.mult,
            )

        def tout(b, j, bank):
            acc = bank_tile(("o", 4 * b + j), bank, [P, DIM])
            for c in range(4):
                nc.tensor.transpose(out=acc[:, c * P:(c + 1) * P], in_=live[("ot", b)][:, c, j * P:(j + 1) * P], identity=ident[:])

        def ev(b, j, engine):
            o = ring_tile(("osb", b), [P, PACK, DIM], F32, "osb", OSB_BUFS)
            if engine == "ACT":
                nc.scalar.copy(out=o[:, j, :], in_=live[("o", 4 * b + j)][:])
            else:
                nc.vector.tensor_copy(out=o[:, j, :], in_=live[("o", 4 * b + j)][:])

        def store(b, j0, j1):
            nc.sync.dma_start(
                out=of[b * BLK:(b + 1) * BLK, :].rearrange("(p j) d -> p j d", j=PACK)[:, j0:j1, :], in_=live[("osb", b)][:, j0:j1, :]
            )

        step("POOL", "ident", [], lambda: make_identity(nc, ident[:]))
        step("SP", "ld_b1", [], lambda: nc.sync.dma_start(out=b1raw[:], in_=b1.rearrange("(p t) -> p t", t=PACK)))
        step("SP", "ld_x0_0", [], lambda: ld_x(0, 0, 2))
        step("SP", "ld_w1", [], lambda: ld_w_pairs("w1", W1))
        step("SP", "ld_x0_1", [], lambda: ld_x(0, 2, 4))
        for b in range(1, NB):
            step("SP", "ld_x%d" % b, [], lambda b=b: ld_x(b, 0, 4))
        step("SP", "ld_wv", [], lambda: ld_w_pairs("wv", Wv))
        step("SP", "ld_w2", [], lambda: ld_w_rows("w2", W2g))
        step("SP", "ld_bias", ["memsets"], ld_bias)

        step("DVE", "memsets", [], memsets)
        step("ACT", "warm", ["memsets"], lambda: nc.scalar.activation(out=warm[:, 1:2], in_=warm[:, 0:1], func=ACT.Silu))

        def pe_tx(b, jjs=(0, 1)):
            for jj in jjs:
                deps = ["ld_x0_%d" % jj if b == 0 else "ld_x%d" % b, "ident"]
                deps += claim(XT_BANKS[(2 * b + jj) % len(XT_BANKS)], "xc%d_%d" % (b, jj))
                step("PE", "tx%d_%d" % (b, jj), deps, lambda jj=jj: tx(b, jj))

        def pe_mx1(i, ts=(0, 1, 2, 3)):
            for t in ts:
                bank = Z_BANKS[(4 * i + t) % len(Z_BANKS)]
                deps = ["qx%d" % i, "qw1_%d" % t] + claim(bank, "silu%d_%d" % (i, t))
                step("PE", "mx1_%d_%d" % (i, t), deps, lambda t=t, bank=bank: mx(("z", 4 * i + t), bank, "w1", t, xcod, xscl, UNITS1[i]))

        pe_tx(0)
        pe_mx1(0, (0, 1))
        pe_tx(1)
        pe_mx1(0, (2, 3))
        pe_mx1(1)
        pe_tx(2)
        pe_tx(3)
        pe_mx1(2)
        pe_tx(4)
        pe_mx1(3)
        pe_tx(5)
        pe_tx(6)
        pe_mx1(4)
        pe_tx(7)
        pe_mx1(5)
        pe_mx1(6)
        step("PE", "tb", ["cbrow"] + claim(XT_BANKS[0], "cb2"),
             lambda: nc.tensor.transpose(out=bank_tile(("bt", 0), XT_BANKS[0], [P, P])[:], in_=browf[:], identity=ident[:]))
        pe_mx1(7)
        pe_mx1(8)

        def v_xc(b, jj):
            eng = "ACT" if (b, jj) in XC_ON_ACT else "DVE"
            deps = ["tx%d_%d" % (b, jj)] + grp_prev(b)
            step(eng, "xc%d_%d" % (b, jj), deps, lambda: xc(b, jj, eng))

        def v_qx(i):
            b, c0, n = UNITS1[i]
            step("DVE", "qx%d" % i, ["xc%d_%d" % (b, jj) for jj in range(c0 // HALF, (c0 + n) // HALF)], lambda: qx(UNITS1[i]))

        def v_rw1(t):
            step("DVE", "rw1_%d" % t, ["ld_w1"], lambda: regroup_w1(t))

        def v_qw1(t):
            step("DVE", "qw1_%d" % t, ["rw1_%d" % t], lambda: quant_w("w1", t * P, (t + 1) * P))

        step("DVE", "cb1", ["ld_b1"], lambda: nc.vector.tensor_copy(out=b1f[:], in_=b1raw[:]))
        v_xc(0, 0)
        v_xc(0, 1)
        v_rw1(0)
        v_rw1(1)
        v_qw1(0)
        v_qx(0)
        v_rw1(2)
        v_qw1(1)
        v_rw1(3)
        v_qw1(2)
        v_qx(1)
        v_qw1(3)
        v_xc(1, 0)
        v_xc(1, 1)
        v_qx(2)
        v_xc(2, 0)
        v_xc(2, 1)
        for b in range(3, NB):
            v_xc(b, 0)
            v_qx(b)
            v_xc(b, 1)
        step("DVE", "rwv", ["ld_wv"], lambda: regroup_w("wv"))
        v_qx(NB)
        step("DVE", "cbrow", ["ld_bias"], lambda: nc.vector.tensor_copy(out=browf[:], in_=brow[:]))
        step("DVE", "rw2", ["ld_w2"], lambda: regroup_w("w2"))
        step("DVE", "qwv", ["rwv"], lambda: quant_w("wv", 0, DIM))
        step("DVE", "qw2", ["rw2"], lambda: quant_w("w2", 0, DIM))

        def v_hr(b):
            eng = "POOL" if b in HR_ON_POOL else "DVE"
            deps = ["silu%d_%d" % (i, t) for i in range(len(UNITS1)) if UNITS1[i][0] == b for t in range(4)] + grp_prev(NB + b)
            step(eng, "hr%d" % b, deps, lambda: hr(b, eng))

        def v_qh(b):
            step("DVE", "qh%d" % b, ["hr%d" % b], lambda: qh(b))

        for i in range(len(UNITS1)):
            for t in range(4):
                step("ACT", "silu%d_%d" % (i, t), ["mx1_%d_%d" % (i, t), "cb1", "warm"], lambda i=i, t=t: silu(i, t))

        nbank = [0]

        def next_bank(reader):
            bank = nbank[0] % 8
            nbank[0] += 1
            return bank, claim(bank, reader)

        def js_of(i):
            b, c0, n = UNITS2[i]
            return [(b, j) for j in range(c0 // P, (c0 + n) // P)]

        def pe_mx2(i):
            b = UNITS2[i][0]
            for c in range(4):
                bank, war = next_bank("sg%d_%d" % (i, c))
                step("PE", "g%d_%d" % (i, c), ["qh%d" % b, "qw2"] + war, lambda c=c, bank=bank: mx(("g", 4 * i + c), bank, "w2", c, hcod, hscl, UNITS2[i]))
                bank, war = next_bank("st%d_%d" % (i, c))
                step("PE", "v%d_%d" % (i, c), ["qx%d" % (b + 1), "qwv"] + war, lambda c=c, bank=bank: mx(("v", 4 * i + c), bank, "wv", c, xcod, xscl, UNITS2[i]))

        def pe_tout(i):
            for b, j in js_of(i):
                bank, war = next_bank("ev%d_%d" % (b, j))
                step("PE", "to%d_%d" % (b, j), ["st%d_%d" % (i, c) for c in range(4)] + war, lambda b=b, j=j, bank=bank: tout(b, j, bank))

        pe_mx2(0)
        for i in range(1, len(UNITS2)):
            pe_mx2(i)
            pe_tout(i - 1)
        pe_tout(len(UNITS2) - 1)

        def a_sg(i, c):
            n = 4 * i + c - SIG_BUFS
            deps = ["g%d_%d" % (i, c), "cb2"] + (["st%d_%d" % (n // 4, n % 4)] if n >= 0 else [])
            step("ACT", "sg%d_%d" % (i, c), deps, lambda: sg(i, c))

        store_names = dict((b, []) for b in range(NB))

        def any_ev(b, j):
            eng = "DVE" if (b, j) in EV_ON_DVE else "ACT"
            deps = ["to%d_%d" % (b, j)] + (store_names[b - OSB_BUFS] if b >= OSB_BUFS else [])
            step(eng, "ev%d_%d" % (b, j), deps, lambda: ev(b, j, eng))

        def v_st(i, c):
            b = UNITS2[i][0]
            deps = ["v%d_%d" % (i, c), "sg%d_%d" % (i, c)] + (["to%d_%d" % (b - OT_BUFS, j) for j in range(4)] if b >= OT_BUFS else [])
            step("DVE", "st%d_%d" % (i, c), deps, lambda: st(i, c))

        def stores(i):
            js = js_of(i)
            width = 1 if i == len(UNITS2) - 1 else 2
            for k in range(0, len(js), width):
                b, j = js[k]
                name = "store%d_%d" % (b, j)
                store_names[b].append(name)
                step("SP", name, ["ev%d_%d" % (b, j + d) for d in range(width)], lambda b=b, j=j: store(b, j, j + width))

        v_hr(0)
        for b in range(1, H_EARLY):
            v_hr(b)
            v_qh(b - 1)
            if b == 1:
                step("DVE", "cb2", ["tb"], lambda: nc.vector.tensor_copy(out=b2v[:], in_=live[("bt", 0)][:, 0:8]))
        v_qh(H_EARLY - 1)
        for i in range(len(UNITS2) + 1):
            nxt = i + H_EARLY
            if i < len(UNITS2):
                for c in range(4):
                    a_sg(i, c)
                    v_st(i, c)
            if nxt < NB:
                v_hr(nxt)
            if i >= 1:
                for b, j in js_of(i - 1):
                    any_ev(b, j)
            if nxt < NB:
                v_qh(nxt)
            if i >= 1:
                stores(i - 1)

        done = set()
        heads = dict((e, 0) for e in order)
        left = sum(len(v) for v in order.values())
        while left:
            moved = 0
            for e in ("SP", "POOL", "PE", "DVE", "ACT"):
                while heads[e] < len(order[e]):
                    name = order[e][heads[e]]
                    deps, fn = steps[name]
                    if not all(d in done for d in deps):
                        break
                    fn()
                    done.add(name)
                    heads[e] += 1
                    moved += 1
            assert moved, "the orders wait for each other: %s" % [order[e][heads[e]] for e in order if heads[e] < len(order[e])]
            left -= moved
